import numpy as np
import ml_dtypes


def mxq(x, axis, fmt="e4m3"):
    dtype, down = {"e4m3": (ml_dtypes.float8_e4m3fn, 7), "e5m2": (ml_dtypes.float8_e5m2, 14)}[fmt]
    v = np.moveaxis(np.asarray(x, np.float32).astype(ml_dtypes.bfloat16).astype(np.float64), axis, -1)
    blocks = v.reshape(v.shape[:-1] + (-1, 32))
    amax = np.abs(blocks).max(-1, keepdims=True)
    byte = np.maximum(np.where(amax > 0, np.frexp(amax)[1] - 1 + 127, 0) - down, 1)
    scale = np.exp2(byte - 127.0)
    codes = (blocks / scale).astype(np.float32).astype(dtype).astype(np.float64)
    return np.moveaxis((codes * scale).reshape(v.shape), -1, axis)


WIDE = False


def mx_kscale(k):
    if not WIDE:
        return np.ones(k)
    levels = np.array([10, -10, 5, -5, 0])
    if k % 512:
        return np.exp2(np.random.permutation(np.resize(levels, k // 32))).repeat(32)
    a = np.empty((k // 512, 16))
    for p in range(k // 512):
        a[p, :8] = np.random.permutation(np.resize(levels, 8))
        for g in range(8):
            far = levels[np.abs(levels - a[p, g]) >= 10]
            a[p, g + 8] = far[np.random.randint(len(far))]
    return np.exp2(a.ravel()).repeat(32)


BF16 = ml_dtypes.bfloat16


def bf(x):
    return np.asarray(x, np.float32).astype(BF16)


def f64(x):
    return np.asarray(x).astype(np.float64)


B, D_IN, D_H = 512, 1024, 1024


def sigmoid(v):
    return 1.0 / (1.0 + np.exp(-v))


def setup_inputs():
    s, t = mx_kscale(D_IN), mx_kscale(D_H)

    def w_in():
        return bf(np.random.standard_normal((D_H, D_IN)) * 0.6 / np.sqrt(D_IN) / s[None, :])

    def w_rec():
        return bf(np.random.standard_normal((D_H, D_H)) * 0.6 / np.sqrt(D_H) / t[None, :])

    def bias():
        return bf(np.random.standard_normal(D_H) * 0.3)

    return {"incoming": bf(np.random.standard_normal((B, D_IN)) * s), "h": bf(np.random.standard_normal((B, D_H)) * t),
            "W_i": w_in(), "b_W_i": bias(), "W_c": w_in(), "b_W_c": bias(),
            "U_i": w_rec(), "b_U_i": bias(), "U_c": w_rec(), "b_U_c": bias()}


def reference(incoming, h, W_i, b_W_i, W_c, b_W_c, U_i, b_U_i, U_c, b_U_c):
    xq = mxq(f64(incoming), 1, "e4m3")
    hq = mxq(f64(h), 1, "e4m3")
    I = sigmoid((xq @ mxq(f64(W_i), 1, "e4m3").T) + f64(b_W_i) + (hq @ mxq(f64(U_i), 1, "e4m3").T) + f64(b_U_i))
    C_head = (xq @ mxq(f64(W_c), 1, "e4m3").T) + f64(b_W_c) + (hq @ mxq(f64(U_c), 1, "e4m3").T) + f64(b_U_c)
    return I * C_head

@@ -1,0 +1,210 @@
+from contextlib import ExitStack
+
+import concourse.mybir as mybir
+from concourse.masks import make_identity
+
+F32 = mybir.dt.float32
+BF16 = mybir.dt.bfloat16
+U32 = mybir.dt.uint32
+U8 = mybir.dt.uint8
+FP8X4 = mybir.dt.float8_e4m3fn_x4
+SIGMOID = mybir.ActivationFunctionType.Sigmoid
+ADD = mybir.AluOpType.add
+MULT = mybir.AluOpType.mult
+
+P = 128
+PACK = 4
+BATCH = 512
+FEATURES = 1024
+OUTPUTS = 1024
+PASSES = FEATURES // (P * PACK)
+WORD_BLOCKS = FEATURES // 2 // P
+BATCH_TILES = BATCH // P
+UNITS = OUTPUTS // P
+SOURCES = 2
+GATES = 2
+BLOCK = 32
+
+FLOPS = 2 * BATCH * OUTPUTS * FEATURES * SOURCES * GATES
+
+
+def tile_lstmcell_pa_kernel(
+    tc, incoming, h, W_i, b_W_i, W_c, b_W_c, U_i, b_U_i, U_c, b_U_c, out
+):
+    nc = tc.nc
+    activations = (incoming, h)
+    weights = (W_i, U_i, W_c, U_c)
+    biases = (b_W_i, b_U_i, b_W_c, b_U_c)
+
+    with ExitStack() as ctx:
+        ctx.enter_context(tc.manual_schedule())
+
+        const = ctx.enter_context(tc.tile_pool(name="const", bufs=1))
+        act_rows_pool = ctx.enter_context(tc.tile_pool(name="act_rows", bufs=SOURCES))
+        w_rows_pool = ctx.enter_context(tc.tile_pool(name="w_rows", bufs=UNITS))
+        act_grouped_pool = ctx.enter_context(tc.tile_pool(name="act_grouped", bufs=SOURCES))
+        w_grouped_pool = ctx.enter_context(tc.tile_pool(name="w_grouped", bufs=2))
+        w_mx_pool = ctx.enter_context(tc.tile_pool(name="w_mx", bufs=2))
+        result_pool = ctx.enter_context(tc.tile_pool(name="result", bufs=3))
+        word_banks = ctx.enter_context(tc.psum_pool(name="word_banks", bufs=6))
+        sum_banks = ctx.enter_context(tc.psum_pool(name="sum_banks", bufs=1))
+
+        act_rows = []
+        for source in range(SOURCES):
+            rows = act_rows_pool.tile([P, BATCH_TILES, FEATURES], BF16, name="act_rows")
+            for bt in range(BATCH_TILES):
+                nc.sync.dma_start(
+                    out=rows[:, bt, :], in_=activations[source][bt * P : (bt + 1) * P, :]
+                )
+            act_rows.append(rows)
+        w_rows = []
+        for unit in range(UNITS):
+            rows = w_rows_pool.tile([P, len(weights), FEATURES], BF16, name="w_rows")
+            for m in range(len(weights)):
+                nc.sync.dma_start(
+                    out=rows[:, m, :], in_=weights[m][unit * P : (unit + 1) * P, :]
+                )
+            w_rows.append(rows)
+
+        bias_rows = const.tile([P, P], BF16, name="bias_rows")
+        nc.vector.memset(bias_rows[:], 0.0)
+        for m in range(len(biases)):
+            nc.scalar.dma_start(
+                out=bias_rows[m * UNITS : (m + 1) * UNITS, :],
+                in_=biases[m].rearrange("(u p) -> u p", p=P),
+            )
+
+        identity = const.tile([P, P], F32, name="identity")
+        make_identity(nc, identity[:])
+
+        warm = const.tile([P, 2], F32, name="warm")
+        nc.vector.memset(warm[:], 0.0)
+        nc.scalar.activation(out=warm[:, 1:2], in_=warm[:, 0:1], func=SIGMOID)
+
+        def transpose_rows(rows_bf16, grouped_words, copy):
+            words = rows_bf16.bitcast(F32)
+            bank = word_banks.tile([P, WORD_BLOCKS, P], F32, name="bank")
+            for v in range(WORD_BLOCKS):
+                g, u = v // 2, v % 2
+                nc.tensor.transpose(
+                    bank[:, v, :], words[:, 2 * P * g + u : 2 * P * (g + 1) : 2], identity[:]
+                )
+            copy(out=grouped_words, in_=bank[:].rearrange("p (g u) r -> p g r u", u=2))
+
+        act_codes = const.tile([P, SOURCES, PASSES, BATCH], U32, name="act_codes", align_bytes=64)
+        act_scales = const.tile([P, SOURCES, PASSES, BATCH], U8, name="act_scales", align_bytes=64)
+        for source in range(SOURCES):
+            grouped = act_grouped_pool.tile(
+                [P, PASSES, BATCH, PACK], BF16, name="act_grouped", align_bytes=64
+            )
+            grouped_words = grouped[:].bitcast(F32)
+            for bt in range(BATCH_TILES):
+                transpose_rows(
+                    act_rows[source][:, bt, :],
+                    grouped_words[:, :, bt * P : (bt + 1) * P, :],
+                    nc.vector.tensor_copy if bt % 2 == 0 else nc.scalar.copy,
+                )
+            nc.vector.quantize_mx(
+                out=act_codes[:, source].rearrange("p g b -> p (g b)").bitcast(FP8X4),
+                scales=act_scales[:, source].rearrange("p g b -> p (g b)"),
+                in_=grouped[:].rearrange("p g b t -> p (g b t)"),
+            )
+
+        def transpose_unit(unit):
+            grouped = w_grouped_pool.tile(
+                [P, len(weights), PASSES, P, PACK], BF16, name="w_grouped", align_bytes=64
+            )
+            grouped_words = grouped[:].bitcast(F32)
+            for m in range(len(weights)):
+                transpose_rows(w_rows[unit][:, m, :], grouped_words[:, m], nc.scalar.copy)
+            return grouped
+
+        def quantise_unit(grouped):
+            codes = w_mx_pool.tile(
+                [P, len(weights), PASSES, P], U32, name="w_codes", align_bytes=64
+            )
+            scales = w_mx_pool.tile(
+                [P, len(weights), PASSES, P], U8, name="w_scales", align_bytes=64
+            )
+            for gate in range(GATES):
+                pair = slice(SOURCES * gate, SOURCES * (gate + 1))
+                nc.vector.quantize_mx(
+                    out=codes[:, pair].rearrange("p m g r -> p (m g r)").bitcast(FP8X4),
+                    scales=scales[:, pair].rearrange("p m g r -> p (m g r)"),
+                    in_=grouped[:, pair].rearrange("p m g r t -> p (m g r t)"),
+                )
+            return codes, scales
+
+        def multiply(sums, gate, codes, scales):
+            steps = [(source, g) for source in range(SOURCES) for g in range(PASSES)]
+            for source, g in steps:
+                m = SOURCES * gate + source
+                nc.tensor.matmul_mx(
+                    out=sums[:],
+                    lhsT=codes[:, m, g, :].bitcast(FP8X4),
+                    lhsT_scale=scales[:, m, g, :],
+                    rhs=act_codes[:, source, g, :].bitcast(FP8X4),
+                    rhs_scale=act_scales[:, source, g, :],
+                    start=(source, g) == steps[0],
+                    stop=(source, g) == steps[-1],
+                )
+
+        def store_product(unit, product):
+            turned = result_pool.tile([P, BATCH], F32, name="turned", align_bytes=64)
+            nc.vector.transpose(out=turned[:], in_=product[:])
+            for a in range(P // BLOCK):
+                first = unit * P + a * BLOCK
+                nc.sync.dma_start(
+                    out=out.rearrange("(c i) n -> i c n", i=BLOCK)[:, :, first : first + BLOCK],
+                    in_=turned[a * BLOCK : (a + 1) * BLOCK, :].rearrange(
+                        "i (c j) -> i c j", j=BLOCK
+                    ),
+                )
+
+        first_grouped = transpose_unit(0)
+
+        bias_rows_f32 = const.tile([P, P], F32, name="bias_rows_f32")
+        nc.vector.tensor_copy(out=bias_rows_f32[:], in_=bias_rows[:])
+        bias_bank = word_banks.tile([P, WORD_BLOCKS, P], F32, name="bank")
+        nc.tensor.transpose(bias_bank[:, 0, :], bias_rows_f32[:], identity[:])
+        bias_columns = const.tile([P, GATES, SOURCES, UNITS], F32, name="bias_columns")
+        nc.vector.tensor_copy(
+            out=bias_columns[:].rearrange("p g s u -> p (g s u)"),
+            in_=bias_bank[:, 0, 0 : len(biases) * UNITS],
+        )
+        bias = const.tile([P, GATES, UNITS], F32, name="bias")
+        nc.vector.tensor_tensor(
+            out=bias[:], in0=bias_columns[:, :, 0, :], in1=bias_columns[:, :, 1, :], op=ADD
+        )
+
+        mx_operands = quantise_unit(first_grouped)
+        product = None
+        for unit in range(UNITS):
+            last_product = product
+            if unit + 1 < UNITS:
+                next_grouped = transpose_unit(unit + 1)
+
+            codes, scales = mx_operands
+            gate_sums = sum_banks.tile([P, BATCH], F32, name="gate_sums")
+            multiply(gate_sums, 0, codes, scales)
+            gate = result_pool.tile([P, BATCH], F32, name="gate")
+            nc.scalar.activation(
+                out=gate[:], in_=gate_sums[:], func=SIGMOID, bias=bias[:, 0, unit : unit + 1]
+            )
+            candidate_sums = sum_banks.tile([P, BATCH], F32, name="candidate_sums")
+            multiply(candidate_sums, 1, codes, scales)
+
+            if last_product is not None:
+                store_product(unit - 1, last_product)
+            if unit + 1 < UNITS:
+                mx_operands = quantise_unit(next_grouped)
+            product = result_pool.tile([P, BATCH], F32, name="product", align_bytes=64)
+            nc.vector.scalar_tensor_tensor(
+                out=product[:],
+                in0=candidate_sums[:],
+                scalar=bias[:, 1, unit : unit + 1],
+                in1=gate[:],
+                op0=ADD,
+                op1=MULT,
+            )
+        store_product(UNITS - 1, product)

@@ -43,6 +43,7 @@ def tile_lstmcell_pa_kernel(
         act_rows_pool = ctx.enter_context(tc.tile_pool(name="act_rows", bufs=SOURCES))
         w_rows_pool = ctx.enter_context(tc.tile_pool(name="w_rows", bufs=UNITS))
         act_grouped_pool = ctx.enter_context(tc.tile_pool(name="act_grouped", bufs=SOURCES))
+        w_ordered_pool = ctx.enter_context(tc.tile_pool(name="w_ordered", bufs=2))
         w_grouped_pool = ctx.enter_context(tc.tile_pool(name="w_grouped", bufs=2))
         w_mx_pool = ctx.enter_context(tc.tile_pool(name="w_mx", bufs=2))
         result_pool = ctx.enter_context(tc.tile_pool(name="result", bufs=3))
@@ -81,14 +82,18 @@ def tile_lstmcell_pa_kernel(
         nc.vector.memset(warm[:], 0.0)
         nc.scalar.activation(out=warm[:, 1:2], in_=warm[:, 0:1], func=SIGMOID)
 
-        def transpose_rows(rows_bf16, grouped_words, copy):
+        def every_second_word(rows_bf16):
             words = rows_bf16.bitcast(F32)
+            return [
+                words[:, 2 * P * g + u : 2 * P * (g + 1) : 2]
+                for g in range(PASSES)
+                for u in range(2)
+            ]
+
+        def transpose_blocks(blocks, grouped_words, copy):
             bank = word_banks.tile([P, WORD_BLOCKS, P], F32, name="bank")
             for v in range(WORD_BLOCKS):
-                g, u = v // 2, v % 2
-                nc.tensor.transpose(
-                    bank[:, v, :], words[:, 2 * P * g + u : 2 * P * (g + 1) : 2], identity[:]
-                )
+                nc.tensor.transpose(bank[:, v, :], blocks[v], identity[:])
             copy(out=grouped_words, in_=bank[:].rearrange("p (g u) r -> p g r u", u=2))
 
         act_codes = const.tile([P, SOURCES, PASSES, BATCH], U32, name="act_codes", align_bytes=64)
@@ -99,8 +104,8 @@ def tile_lstmcell_pa_kernel(
             )
             grouped_words = grouped[:].bitcast(F32)
             for bt in range(BATCH_TILES):
-                transpose_rows(
-                    act_rows[source][:, bt, :],
+                transpose_blocks(
+                    every_second_word(act_rows[source][:, bt, :]),
                     grouped_words[:, :, bt * P : (bt + 1) * P, :],
                     nc.vector.tensor_copy if bt % 2 == 0 else nc.scalar.copy,
                 )
@@ -110,13 +115,27 @@ def tile_lstmcell_pa_kernel(
                 in_=grouped[:].rearrange("p g b t -> p (g b t)"),
             )
 
-        def transpose_unit(unit):
+        def order_unit(unit):
+            ordered = w_ordered_pool.tile([P, len(weights), PASSES, 2, P], F32, name="w_ordered")
+            words = w_rows[unit][:].rearrange("r m k -> r (m k)").bitcast(F32)
+            for u in range(2):
+                nc.vector.tensor_copy(
+                    out=ordered[:, :, :, u, :].rearrange("r m g p -> r (m g) p"),
+                    in_=words.rearrange("r (n p u) -> r n p u", p=P, u=2)[:, :, :, u],
+                )
+            return ordered
+
+        def transpose_unit(unit, ordered=None):
             grouped = w_grouped_pool.tile(
                 [P, len(weights), PASSES, P, PACK], BF16, name="w_grouped", align_bytes=64
             )
             grouped_words = grouped[:].bitcast(F32)
             for m in range(len(weights)):
-                transpose_rows(w_rows[unit][:, m, :], grouped_words[:, m], nc.scalar.copy)
+                if ordered is None:
+                    blocks = every_second_word(w_rows[unit][:, m, :])
+                else:
+                    blocks = [ordered[:, m, g, u, :] for g in range(PASSES) for u in range(2)]
+                transpose_blocks(blocks, grouped_words[:, m], nc.scalar.copy)
             return grouped
 
         def quantise_unit(grouped):
@@ -179,10 +198,13 @@ def tile_lstmcell_pa_kernel(
 
         mx_operands = quantise_unit(first_grouped)
         product = None
+        next_ordered = None
         for unit in range(UNITS):
             last_product = product
             if unit + 1 < UNITS:
-                next_grouped = transpose_unit(unit + 1)
+                next_grouped = transpose_unit(unit + 1, next_ordered)
+            if unit + 2 < UNITS:
+                next_ordered = order_unit(unit + 2)
 
             codes, scales = mx_operands
             gate_sums = sum_banks.tile([P, BATCH], F32, name="gate_sums")

@@ -22,7 +22,9 @@ WORD_BLOCKS = FEATURES // 2 // P
 BATCH_TILES = BATCH // P
 UNITS = OUTPUTS // P
 SOURCES = 2
+HALVES = 2
 GATES = 2
+VECTOR_ORDERS = 3
 BLOCK = 32
 
 FLOPS = 2 * BATCH * OUTPUTS * FEATURES * SOURCES * GATES
@@ -42,7 +44,7 @@ def tile_lstmcell_pa_kernel(
         const = ctx.enter_context(tc.tile_pool(name="const", bufs=1))
         act_rows_pool = ctx.enter_context(tc.tile_pool(name="act_rows", bufs=SOURCES))
         w_rows_pool = ctx.enter_context(tc.tile_pool(name="w_rows", bufs=UNITS))
-        act_grouped_pool = ctx.enter_context(tc.tile_pool(name="act_grouped", bufs=SOURCES))
+        act_grouped_pool = ctx.enter_context(tc.tile_pool(name="act_grouped", bufs=SOURCES * HALVES))
         w_ordered_pool = ctx.enter_context(tc.tile_pool(name="w_ordered", bufs=2))
         w_grouped_pool = ctx.enter_context(tc.tile_pool(name="w_grouped", bufs=2))
         w_mx_pool = ctx.enter_context(tc.tile_pool(name="w_mx", bufs=2))
@@ -98,61 +100,75 @@ def tile_lstmcell_pa_kernel(
 
         act_codes = const.tile([P, SOURCES, PASSES, BATCH], U32, name="act_codes", align_bytes=64)
         act_scales = const.tile([P, SOURCES, PASSES, BATCH], U8, name="act_scales", align_bytes=64)
-        for source in range(SOURCES):
-            grouped = act_grouped_pool.tile(
-                [P, PASSES, BATCH, PACK], BF16, name="act_grouped", align_bytes=64
-            )
-            grouped_words = grouped[:].bitcast(F32)
-            for bt in range(BATCH_TILES):
-                transpose_blocks(
-                    every_second_word(act_rows[source][:, bt, :]),
-                    grouped_words[:, :, bt * P : (bt + 1) * P, :],
-                    nc.vector.tensor_copy if bt % 2 == 0 else nc.scalar.copy,
+
+        def prepare_activation(source):
+            for half in range(HALVES):
+                grouped = act_grouped_pool.tile(
+                    [P, PASSES, BATCH // HALVES, PACK], BF16, name="act_grouped", align_bytes=64
                 )
-            nc.vector.quantize_mx(
-                out=act_codes[:, source].rearrange("p g b -> p (g b)").bitcast(FP8X4),
-                scales=act_scales[:, source].rearrange("p g b -> p (g b)"),
-                in_=grouped[:].rearrange("p g b t -> p (g b t)"),
-            )
+                grouped_words = grouped[:].bitcast(F32)
+                for i in range(BATCH_TILES // HALVES):
+                    bt = half * (BATCH_TILES // HALVES) + i
+                    transpose_blocks(
+                        every_second_word(act_rows[source][:, bt, :]),
+                        grouped_words[:, :, i * P : (i + 1) * P, :],
+                        nc.vector.tensor_copy if bt == 0 else nc.scalar.copy,
+                    )
+                columns = slice(half * BATCH // HALVES, (half + 1) * BATCH // HALVES)
+                for g in range(PASSES):
+                    nc.vector.quantize_mx(
+                        out=act_codes[:, source, g, columns].bitcast(FP8X4),
+                        scales=act_scales[:, source, g, columns],
+                        in_=grouped[:, g].rearrange("p b t -> p (b t)"),
+                    )
+
+        prepare_activation(0)
+
+        bias_rows_f32 = const.tile([P, P], F32, name="bias_rows_f32")
+        nc.vector.tensor_copy(out=bias_rows_f32[:], in_=bias_rows[:])
+
+        prepare_activation(1)
 
         def order_unit(unit):
             ordered = w_ordered_pool.tile([P, len(weights), PASSES, 2, P], F32, name="w_ordered")
-            words = w_rows[unit][:].rearrange("r m k -> r (m k)").bitcast(F32)
-            for u in range(2):
-                nc.vector.tensor_copy(
-                    out=ordered[:, :, :, u, :].rearrange("r m g p -> r (m g) p"),
-                    in_=words.rearrange("r (n p u) -> r n p u", p=P, u=2)[:, :, :, u],
-                )
+            order_weights(unit, ordered, slice(0, VECTOR_ORDERS), nc.vector.tensor_copy)
             return ordered
 
-        def transpose_unit(unit, ordered=None):
-            grouped = w_grouped_pool.tile(
-                [P, len(weights), PASSES, P, PACK], BF16, name="w_grouped", align_bytes=64
+        def order_weights(unit, ordered, which, copy):
+            words = w_rows[unit][:, which].rearrange("r m k -> r (m k)").bitcast(F32)
+            copy(
+                out=ordered[:, which].rearrange("r m g u p -> r (m g) u p"),
+                in_=words.rearrange("r (n p u) -> r n u p", p=P, u=2),
             )
+
+        def transpose_gate(unit, gate, grouped, ordered=None):
             grouped_words = grouped[:].bitcast(F32)
-            for m in range(len(weights)):
+            for m in range(SOURCES * gate, SOURCES * (gate + 1)):
                 if ordered is None:
                     blocks = every_second_word(w_rows[unit][:, m, :])
                 else:
                     blocks = [ordered[:, m, g, u, :] for g in range(PASSES) for u in range(2)]
                 transpose_blocks(blocks, grouped_words[:, m], nc.scalar.copy)
-            return grouped
 
-        def quantise_unit(grouped):
+        def new_unit():
+            grouped = w_grouped_pool.tile(
+                [P, len(weights), PASSES, P, PACK], BF16, name="w_grouped", align_bytes=64
+            )
             codes = w_mx_pool.tile(
                 [P, len(weights), PASSES, P], U32, name="w_codes", align_bytes=64
             )
             scales = w_mx_pool.tile(
                 [P, len(weights), PASSES, P], U8, name="w_scales", align_bytes=64
             )
-            for gate in range(GATES):
-                pair = slice(SOURCES * gate, SOURCES * (gate + 1))
-                nc.vector.quantize_mx(
-                    out=codes[:, pair].rearrange("p m g r -> p (m g r)").bitcast(FP8X4),
-                    scales=scales[:, pair].rearrange("p m g r -> p (m g r)"),
-                    in_=grouped[:, pair].rearrange("p m g r t -> p (m g r t)"),
-                )
-            return codes, scales
+            return grouped, codes, scales
+
+        def quantise_gate(gate, grouped, codes, scales):
+            pair = slice(SOURCES * gate, SOURCES * (gate + 1))
+            nc.vector.quantize_mx(
+                out=codes[:, pair].rearrange("p m g r -> p (m g r)").bitcast(FP8X4),
+                scales=scales[:, pair].rearrange("p m g r -> p (m g r)"),
+                in_=grouped[:, pair].rearrange("p m g r t -> p (m g r t)"),
+            )
 
         def multiply(sums, gate, codes, scales):
             steps = [(source, g) for source in range(SOURCES) for g in range(PASSES)]
@@ -180,10 +196,10 @@ def tile_lstmcell_pa_kernel(
                     ),
                 )
 
-        first_grouped = transpose_unit(0)
-
-        bias_rows_f32 = const.tile([P, P], F32, name="bias_rows_f32")
-        nc.vector.tensor_copy(out=bias_rows_f32[:], in_=bias_rows[:])
+        this_unit = new_unit()
+        for gate in range(GATES):
+            transpose_gate(0, gate, this_unit[0])
+            quantise_gate(gate, *this_unit)
         bias_bank = word_banks.tile([P, WORD_BLOCKS, P], F32, name="bank")
         nc.tensor.transpose(bias_bank[:, 0, :], bias_rows_f32[:], identity[:])
         bias_columns = const.tile([P, GATES, SOURCES, UNITS], F32, name="bias_columns")
@@ -196,37 +212,52 @@ def tile_lstmcell_pa_kernel(
             out=bias[:], in0=bias_columns[:, :, 0, :], in1=bias_columns[:, :, 1, :], op=ADD
         )
 
-        mx_operands = quantise_unit(first_grouped)
+        next_unit = new_unit()
+        transpose_gate(1, 0, next_unit[0])
+        quantise_gate(0, *next_unit)
+
         product = None
         next_ordered = None
         for unit in range(UNITS):
             last_product = product
-            if unit + 1 < UNITS:
-                next_grouped = transpose_unit(unit + 1, next_ordered)
+            if unit >= 1 and unit + 1 < UNITS:
+                next_unit = new_unit()
+                for gate in range(GATES):
+                    transpose_gate(unit + 1, gate, next_unit[0], next_ordered)
             if unit + 2 < UNITS:
                 next_ordered = order_unit(unit + 2)
 
-            codes, scales = mx_operands
+            grouped, codes, scales = this_unit
             gate_sums = sum_banks.tile([P, BATCH], F32, name="gate_sums")
             multiply(gate_sums, 0, codes, scales)
-            gate = result_pool.tile([P, BATCH], F32, name="gate")
+            gate_tile = result_pool.tile([P, BATCH], F32, name="gate_tile")
             nc.scalar.activation(
-                out=gate[:], in_=gate_sums[:], func=SIGMOID, bias=bias[:, 0, unit : unit + 1]
+                out=gate_tile[:], in_=gate_sums[:], func=SIGMOID, bias=bias[:, 0, unit : unit + 1]
             )
+            if unit + 2 < UNITS:
+                order_weights(
+                    unit + 2, next_ordered, slice(VECTOR_ORDERS, len(weights)), nc.scalar.copy
+                )
             candidate_sums = sum_banks.tile([P, BATCH], F32, name="candidate_sums")
             multiply(candidate_sums, 1, codes, scales)
+            if unit == 0:
+                transpose_gate(1, 1, next_unit[0])
 
             if last_product is not None:
                 store_product(unit - 1, last_product)
-            if unit + 1 < UNITS:
-                mx_operands = quantise_unit(next_grouped)
+            if 1 <= unit < UNITS - 1:
+                for gate in range(GATES):
+                    quantise_gate(gate, *next_unit)
             product = result_pool.tile([P, BATCH], F32, name="product", align_bytes=64)
             nc.vector.scalar_tensor_tensor(
                 out=product[:],
                 in0=candidate_sums[:],
                 scalar=bias[:, 1, unit : unit + 1],
-                in1=gate[:],
+                in1=gate_tile[:],
                 op0=ADD,
                 op1=MULT,
             )
+            if unit == 0:
+                quantise_gate(1, *next_unit)
+            this_unit = next_unit
         store_product(UNITS - 1, product)

@@ -212,40 +212,35 @@ def tile_lstmcell_pa_kernel(
             out=bias[:], in0=bias_columns[:, :, 0, :], in1=bias_columns[:, :, 1, :], op=ADD
         )
 
-        next_unit = new_unit()
-        transpose_gate(1, 0, next_unit[0])
-        quantise_gate(0, *next_unit)
-
         product = None
         next_ordered = None
         for unit in range(UNITS):
             last_product = product
-            if unit >= 1 and unit + 1 < UNITS:
+            ordered = next_ordered
+            codes, scales = this_unit[1:]
+            if unit + 1 < UNITS:
                 next_unit = new_unit()
-                for gate in range(GATES):
-                    transpose_gate(unit + 1, gate, next_unit[0], next_ordered)
+                transpose_gate(unit + 1, 0, next_unit[0], ordered)
             if unit + 2 < UNITS:
                 next_ordered = order_unit(unit + 2)
-
-            grouped, codes, scales = this_unit
             gate_sums = sum_banks.tile([P, BATCH], F32, name="gate_sums")
             multiply(gate_sums, 0, codes, scales)
             gate_tile = result_pool.tile([P, BATCH], F32, name="gate_tile")
             nc.scalar.activation(
                 out=gate_tile[:], in_=gate_sums[:], func=SIGMOID, bias=bias[:, 0, unit : unit + 1]
             )
+            if unit + 1 < UNITS:
+                transpose_gate(unit + 1, 1, next_unit[0], ordered)
             if unit + 2 < UNITS:
                 order_weights(
                     unit + 2, next_ordered, slice(VECTOR_ORDERS, len(weights)), nc.scalar.copy
                 )
             candidate_sums = sum_banks.tile([P, BATCH], F32, name="candidate_sums")
             multiply(candidate_sums, 1, codes, scales)
-            if unit == 0:
-                transpose_gate(1, 1, next_unit[0])
 
             if last_product is not None:
                 store_product(unit - 1, last_product)
-            if 1 <= unit < UNITS - 1:
+            if unit + 1 < UNITS:
                 for gate in range(GATES):
                     quantise_gate(gate, *next_unit)
             product = result_pool.tile([P, BATCH], F32, name="product", align_bytes=64)
@@ -257,7 +252,5 @@ def tile_lstmcell_pa_kernel(
                 op0=ADD,
                 op1=MULT,
             )
-            if unit == 0:
-                quantise_gate(1, *next_unit)
             this_unit = next_unit
         store_product(UNITS - 1, product)

@@ -25,7 +25,6 @@ SOURCES = 2
 HALVES = 2
 GATES = 2
 VECTOR_ORDERS = 3
-BLOCK = 32
 
 FLOPS = 2 * BATCH * OUTPUTS * FEATURES * SOURCES * GATES
 
@@ -184,17 +183,19 @@ def tile_lstmcell_pa_kernel(
                     stop=(source, g) == steps[-1],
                 )
 
-        def store_product(unit, product):
-            turned = result_pool.tile([P, BATCH], F32, name="turned", align_bytes=64)
-            nc.vector.transpose(out=turned[:], in_=product[:])
-            for a in range(P // BLOCK):
-                first = unit * P + a * BLOCK
-                nc.sync.dma_start(
-                    out=out.rearrange("(c i) n -> i c n", i=BLOCK)[:, :, first : first + BLOCK],
-                    in_=turned[a * BLOCK : (a + 1) * BLOCK, :].rearrange(
-                        "i (c j) -> i c j", j=BLOCK
-                    ),
-                )
+        def turn_product(product):
+            bank = word_banks.tile([P, WORD_BLOCKS, P], F32, name="bank")
+            for bt in range(BATCH_TILES):
+                nc.tensor.transpose(bank[:, bt, :], product[:, bt * P : (bt + 1) * P], identity[:])
+            return bank
+
+        def store_product(unit, bank):
+            rows = result_pool.tile([P, BATCH_TILES, P], F32, name="rows")
+            nc.vector.tensor_copy(out=rows[:], in_=bank[:])
+            nc.sync.dma_start(
+                out=out.rearrange("(c p) n -> p c n", p=P)[:, :, unit * P : (unit + 1) * P],
+                in_=rows[:],
+            )
 
         this_unit = new_unit()
         for gate in range(GATES):
@@ -231,6 +232,8 @@ def tile_lstmcell_pa_kernel(
             )
             if unit + 1 < UNITS:
                 transpose_gate(unit + 1, 1, next_unit[0], ordered)
+            if last_product is not None:
+                turned_bank = turn_product(last_product)
             if unit + 2 < UNITS:
                 order_weights(
                     unit + 2, next_ordered, slice(VECTOR_ORDERS, len(weights)), nc.scalar.copy
@@ -239,7 +242,7 @@ def tile_lstmcell_pa_kernel(
             multiply(candidate_sums, 1, codes, scales)
 
             if last_product is not None:
-                store_product(unit - 1, last_product)
+                store_product(unit - 1, turned_bank)
             if unit + 1 < UNITS:
                 for gate in range(GATES):
                     quantise_gate(gate, *next_unit)
@@ -253,4 +256,4 @@ def tile_lstmcell_pa_kernel(
                 op1=MULT,
             )
             this_unit = next_unit
-        store_product(UNITS - 1, product)
+        store_product(UNITS - 1, turn_product(product))

@@ -24,6 +24,8 @@ UNITS = OUTPUTS // P
 SOURCES = 2
 HALVES = 2
 GATES = 2
+BLOCK = 32
+VECTOR_TURNS = 4
 VECTOR_ORDERS = 3
 
 FLOPS = 2 * BATCH * OUTPUTS * FEATURES * SOURCES * GATES
@@ -169,32 +171,57 @@ def tile_lstmcell_pa_kernel(
                 in_=grouped[:, pair].rearrange("p m g r t -> p (m g r t)"),
             )
 
-        def multiply(sums, gate, codes, scales):
+        def multiply(sums, gate, codes, scales, columns=slice(0, BATCH)):
             steps = [(source, g) for source in range(SOURCES) for g in range(PASSES)]
             for source, g in steps:
                 m = SOURCES * gate + source
                 nc.tensor.matmul_mx(
-                    out=sums[:],
+                    out=sums,
                     lhsT=codes[:, m, g, :].bitcast(FP8X4),
                     lhsT_scale=scales[:, m, g, :],
-                    rhs=act_codes[:, source, g, :].bitcast(FP8X4),
-                    rhs_scale=act_scales[:, source, g, :],
+                    rhs=act_codes[:, source, g, columns].bitcast(FP8X4),
+                    rhs_scale=act_scales[:, source, g, columns],
                     start=(source, g) == steps[0],
                     stop=(source, g) == steps[-1],
                 )
 
-        def turn_product(product):
+        def form_product(unit, product, candidate_sums, gate_tile):
+            nc.vector.scalar_tensor_tensor(
+                out=product,
+                in0=candidate_sums,
+                scalar=bias[:, 1, unit : unit + 1],
+                in1=gate_tile,
+                op0=ADD,
+                op1=MULT,
+            )
+
+        def turn_on_vector(unit, product):
+            turned = result_pool.tile([P, BATCH], F32, name="turned", align_bytes=64)
+            nc.vector.transpose(out=turned[:], in_=product[:])
+            for a in range(P // BLOCK):
+                first = unit * P + a * BLOCK
+                nc.sync.dma_start(
+                    out=out.rearrange("(c i) n -> i c n", i=BLOCK)[:, :, first : first + BLOCK],
+                    in_=turned[a * BLOCK : (a + 1) * BLOCK, :].rearrange(
+                        "i (c j) -> i c j", j=BLOCK
+                    ),
+                )
+
+        def turn_on_tensor(product, tiles):
             bank = word_banks.tile([P, WORD_BLOCKS, P], F32, name="bank")
-            for bt in range(BATCH_TILES):
-                nc.tensor.transpose(bank[:, bt, :], product[:, bt * P : (bt + 1) * P], identity[:])
+            for i, bt in enumerate(tiles):
+                nc.tensor.transpose(bank[:, i, :], product[:, bt * P : (bt + 1) * P], identity[:])
             return bank
 
-        def store_product(unit, bank):
+        def store_turned(unit, bank, tiles):
+            count = len(tiles)
             rows = result_pool.tile([P, BATCH_TILES, P], F32, name="rows")
-            nc.vector.tensor_copy(out=rows[:], in_=bank[:])
+            nc.vector.tensor_copy(out=rows[:, :count], in_=bank[:, :count])
             nc.sync.dma_start(
-                out=out.rearrange("(c p) n -> p c n", p=P)[:, :, unit * P : (unit + 1) * P],
-                in_=rows[:],
+                out=out.rearrange("(c p) n -> p c n", p=P)[
+                    :, tiles[0] : tiles[0] + count, unit * P : (unit + 1) * P
+                ],
+                in_=rows[:, :count],
             )
 
         this_unit = new_unit()
@@ -213,47 +240,55 @@ def tile_lstmcell_pa_kernel(
             out=bias[:], in0=bias_columns[:, :, 0, :], in1=bias_columns[:, :, 1, :], op=ADD
         )
 
+
         product = None
         next_ordered = None
         for unit in range(UNITS):
+            last = unit == UNITS - 1
             last_product = product
             ordered = next_ordered
             codes, scales = this_unit[1:]
-            if unit + 1 < UNITS:
+            if not last:
                 next_unit = new_unit()
                 transpose_gate(unit + 1, 0, next_unit[0], ordered)
             if unit + 2 < UNITS:
                 next_ordered = order_unit(unit + 2)
             gate_sums = sum_banks.tile([P, BATCH], F32, name="gate_sums")
-            multiply(gate_sums, 0, codes, scales)
+            multiply(gate_sums[:], 0, codes, scales)
             gate_tile = result_pool.tile([P, BATCH], F32, name="gate_tile")
             nc.scalar.activation(
                 out=gate_tile[:], in_=gate_sums[:], func=SIGMOID, bias=bias[:, 0, unit : unit + 1]
             )
-            if unit + 1 < UNITS:
+            if not last:
                 transpose_gate(unit + 1, 1, next_unit[0], ordered)
-            if last_product is not None:
-                turned_bank = turn_product(last_product)
+            if unit > VECTOR_TURNS:
+                turned_bank = turn_on_tensor(last_product, range(BATCH_TILES))
             if unit + 2 < UNITS:
                 order_weights(
                     unit + 2, next_ordered, slice(VECTOR_ORDERS, len(weights)), nc.scalar.copy
                 )
-            candidate_sums = sum_banks.tile([P, BATCH], F32, name="candidate_sums")
-            multiply(candidate_sums, 1, codes, scales)
-
-            if last_product is not None:
-                store_product(unit - 1, turned_bank)
-            if unit + 1 < UNITS:
+            product = result_pool.tile([P, BATCH], F32, name="product", align_bytes=64)
+            if last:
+                half = BATCH // 2
+                for columns, name in (
+                    (slice(0, half), "candidate_sums"),
+                    (slice(half, BATCH), "gate_sums"),
+                ):
+                    sums = sum_banks.tile([P, BATCH], F32, name=name)
+                    multiply(sums[:, :half], 1, codes, scales, columns)
+                    if name == "candidate_sums":
+                        store_turned(unit - 1, turned_bank, range(BATCH_TILES))
+                    form_product(unit, product[:, columns], sums[:, :half], gate_tile[:, columns])
+            else:
+                sums = sum_banks.tile([P, BATCH], F32, name="candidate_sums")
+                multiply(sums[:], 1, codes, scales)
+                if unit > VECTOR_TURNS:
+                    store_turned(unit - 1, turned_bank, range(BATCH_TILES))
+                elif unit > 0:
+                    turn_on_vector(unit - 1, last_product)
                 for gate in range(GATES):
                     quantise_gate(gate, *next_unit)
-            product = result_pool.tile([P, BATCH], F32, name="product", align_bytes=64)
-            nc.vector.scalar_tensor_tensor(
-                out=product[:],
-                in0=candidate_sums[:],
-                scalar=bias[:, 1, unit : unit + 1],
-                in1=gate_tile[:],
-                op0=ADD,
-                op1=MULT,
-            )
-            this_unit = next_unit
-        store_product(UNITS - 1, turn_product(product))
+                form_product(unit, product[:], sums[:], gate_tile[:])
+                this_unit = next_unit
+        for tiles in (range(0, 2), range(2, 4)):
+            store_turned(UNITS - 1, turn_on_tensor(product, tiles), tiles)

@@ -24,8 +24,12 @@ UNITS = OUTPUTS // P
 SOURCES = 2
 HALVES = 2
 GATES = 2
+STEPS = SOURCES * PASSES
+RUN_WEIGHTS = 3
+RUN_PASSES = 6
+STRIDED_UNITS = 2
 BLOCK = 32
-VECTOR_TURNS = 4
+VECTOR_TURNS = 5
 VECTOR_ORDERS = 3
 
 FLOPS = 2 * BATCH * OUTPUTS * FEATURES * SOURCES * GATES
@@ -46,9 +50,10 @@ def tile_lstmcell_pa_kernel(
         act_rows_pool = ctx.enter_context(tc.tile_pool(name="act_rows", bufs=SOURCES))
         w_rows_pool = ctx.enter_context(tc.tile_pool(name="w_rows", bufs=UNITS))
         act_grouped_pool = ctx.enter_context(tc.tile_pool(name="act_grouped", bufs=SOURCES * HALVES))
-        w_ordered_pool = ctx.enter_context(tc.tile_pool(name="w_ordered", bufs=2))
-        w_grouped_pool = ctx.enter_context(tc.tile_pool(name="w_grouped", bufs=2))
-        w_mx_pool = ctx.enter_context(tc.tile_pool(name="w_mx", bufs=2))
+        w_ordered_pool = ctx.enter_context(tc.tile_pool(name="w_ordered", bufs=2 * RUN_WEIGHTS + 2))
+        w_grouped_pool = ctx.enter_context(tc.tile_pool(name="w_grouped", bufs=3))
+        w_mx_pool = ctx.enter_context(tc.tile_pool(name="w_mx", bufs=3))
+        rows_pool = ctx.enter_context(tc.tile_pool(name="rows", bufs=5))
         result_pool = ctx.enter_context(tc.tile_pool(name="result", bufs=3))
         word_banks = ctx.enter_context(tc.psum_pool(name="word_banks", bufs=6))
         sum_banks = ctx.enter_context(tc.psum_pool(name="sum_banks", bufs=1))
@@ -130,26 +135,22 @@ def tile_lstmcell_pa_kernel(
 
         prepare_activation(1)
 
-        def order_unit(unit):
-            ordered = w_ordered_pool.tile([P, len(weights), PASSES, 2, P], F32, name="w_ordered")
-            order_weights(unit, ordered, slice(0, VECTOR_ORDERS), nc.vector.tensor_copy)
-            return ordered
-
-        def order_weights(unit, ordered, which, copy):
-            words = w_rows[unit][:, which].rearrange("r m k -> r (m k)").bitcast(F32)
+        def order_weight(k, copy):
+            unit, m = divmod(k, len(weights))
+            ordered[k] = w_ordered_pool.tile([P, PASSES, 2, P], F32, name="w_ordered")
             copy(
-                out=ordered[:, which].rearrange("r m g u p -> r (m g) u p"),
-                in_=words.rearrange("r (n p u) -> r n u p", p=P, u=2),
+                out=ordered[k][:],
+                in_=w_rows[unit][:, m].bitcast(F32).rearrange("r (g p u) -> r g u p", p=P, u=2),
             )
 
-        def transpose_gate(unit, gate, grouped, ordered=None):
-            grouped_words = grouped[:].bitcast(F32)
-            for m in range(SOURCES * gate, SOURCES * (gate + 1)):
-                if ordered is None:
-                    blocks = every_second_word(w_rows[unit][:, m, :])
-                else:
-                    blocks = [ordered[:, m, g, u, :] for g in range(PASSES) for u in range(2)]
-                transpose_blocks(blocks, grouped_words[:, m], nc.scalar.copy)
+        def transpose_weight(unit, m):
+            grouped = units[unit][0]
+            k = unit * len(weights) + m
+            if k in ordered:
+                blocks = [ordered[k][:, g, u, :] for g in range(PASSES) for u in range(2)]
+            else:
+                blocks = every_second_word(w_rows[unit][:, m, :])
+            transpose_blocks(blocks, grouped[:].bitcast(F32)[:, m], nc.scalar.copy)
 
         def new_unit():
             grouped = w_grouped_pool.tile(
@@ -163,7 +164,8 @@ def tile_lstmcell_pa_kernel(
             )
             return grouped, codes, scales
 
-        def quantise_gate(gate, grouped, codes, scales):
+        def quantise_gate(unit, gate):
+            grouped, codes, scales = units[unit]
             pair = slice(SOURCES * gate, SOURCES * (gate + 1))
             nc.vector.quantize_mx(
                 out=codes[:, pair].rearrange("p m g r -> p (m g r)").bitcast(FP8X4),
@@ -171,19 +173,19 @@ def tile_lstmcell_pa_kernel(
                 in_=grouped[:, pair].rearrange("p m g r t -> p (m g r t)"),
             )
 
-        def multiply(sums, gate, codes, scales, columns=slice(0, BATCH)):
-            steps = [(source, g) for source in range(SOURCES) for g in range(PASSES)]
-            for source, g in steps:
-                m = SOURCES * gate + source
-                nc.tensor.matmul_mx(
-                    out=sums,
-                    lhsT=codes[:, m, g, :].bitcast(FP8X4),
-                    lhsT_scale=scales[:, m, g, :],
-                    rhs=act_codes[:, source, g, columns].bitcast(FP8X4),
-                    rhs_scale=act_scales[:, source, g, columns],
-                    start=(source, g) == steps[0],
-                    stop=(source, g) == steps[-1],
-                )
+        def multiply(sums, unit, gate, step, columns=slice(0, BATCH)):
+            codes, scales = units[unit][1:]
+            source, g = divmod(step, PASSES)
+            m = SOURCES * gate + source
+            nc.tensor.matmul_mx(
+                out=sums,
+                lhsT=codes[:, m, g, :].bitcast(FP8X4),
+                lhsT_scale=scales[:, m, g, :],
+                rhs=act_codes[:, source, g, columns].bitcast(FP8X4),
+                rhs_scale=act_scales[:, source, g, columns],
+                start=step == 0,
+                stop=step == STEPS - 1,
+            )
 
         def form_product(unit, product, candidate_sums, gate_tile):
             nc.vector.scalar_tensor_tensor(
@@ -213,10 +215,10 @@ def tile_lstmcell_pa_kernel(
                 nc.tensor.transpose(bank[:, i, :], product[:, bt * P : (bt + 1) * P], identity[:])
             return bank
 
-        def store_turned(unit, bank, tiles):
+        def store_turned(unit, bank, tiles, copy=nc.vector.tensor_copy):
             count = len(tiles)
-            rows = result_pool.tile([P, BATCH_TILES, P], F32, name="rows")
-            nc.vector.tensor_copy(out=rows[:, :count], in_=bank[:, :count])
+            rows = rows_pool.tile([P, BATCH_TILES, P], F32, name="rows")
+            copy(out=rows[:, :count], in_=bank[:, :count])
             nc.sync.dma_start(
                 out=out.rearrange("(c p) n -> p c n", p=P)[
                     :, tiles[0] : tiles[0] + count, unit * P : (unit + 1) * P
@@ -224,10 +226,23 @@ def tile_lstmcell_pa_kernel(
                 in_=rows[:, :count],
             )
 
-        this_unit = new_unit()
-        for gate in range(GATES):
-            transpose_gate(0, gate, this_unit[0])
-            quantise_gate(gate, *this_unit)
+        units = {}
+        ordered = {}
+        gate_tiles = {}
+        products = {}
+        sums = {}
+        turned_banks = {}
+
+        def next_weight(k):
+            unit, m = divmod(k, len(weights))
+            if m == 0:
+                units[unit] = new_unit()
+            transpose_weight(unit, m)
+
+        for k in range(len(weights)):
+            next_weight(k)
+            if k % 2 == 1:
+                quantise_gate(0, k // 2)
         bias_bank = word_banks.tile([P, WORD_BLOCKS, P], F32, name="bank")
         nc.tensor.transpose(bias_bank[:, 0, :], bias_rows_f32[:], identity[:])
         bias_columns = const.tile([P, GATES, SOURCES, UNITS], F32, name="bias_columns")
@@ -240,55 +255,77 @@ def tile_lstmcell_pa_kernel(
             out=bias[:], in0=bias_columns[:, :, 0, :], in1=bias_columns[:, :, 1, :], op=ADD
         )
 
+        done = len(weights)
+        quantised = GATES
+        passes = UNITS * GATES * STEPS
+        runs = [range(0, STEPS)] + [
+            range(n, min(n + RUN_PASSES, passes)) for n in range(STEPS, passes, RUN_PASSES)
+        ]
+        for run in runs:
+            weights_of_run = RUN_WEIGHTS if run.start > 0 else 4
+            new = range(done, min(done + weights_of_run, UNITS * len(weights)))
+            done = new.stop
+            for k in new:
+                next_weight(k)
+            unit = min(products) if products else UNITS
+            if VECTOR_TURNS <= unit < UNITS - 2:
+                turned_banks[unit] = turn_on_tensor(products[unit], range(BATCH_TILES))
+            soon = [
+                k for k in range(done, min(done + RUN_WEIGHTS, UNITS * len(weights)))
+                if k >= STRIDED_UNITS * len(weights)
+            ]
+            for k in soon:
+                if k % len(weights) < VECTOR_ORDERS:
+                    order_weight(k, nc.vector.tensor_copy)
+            for n in run:
+                unit, gate, step = n // (GATES * STEPS), n // STEPS % GATES, n % STEPS
+                if unit == UNITS - 1 and gate == 1:
+                    break
+                if step == 0:
+                    sums[gate] = sum_banks.tile([P, BATCH], F32, name="sums_%d" % gate)
+                multiply(sums[gate][:], unit, gate, step)
+                if step < STEPS - 1:
+                    continue
+                if gate == 0:
+                    gate_tiles[unit] = result_pool.tile([P, BATCH], F32, name="gate_tile")
+                    nc.scalar.activation(
+                        out=gate_tiles[unit][:],
+                        in_=sums[0][:],
+                        func=SIGMOID,
+                        bias=bias[:, 0, unit : unit + 1],
+                    )
+                else:
+                    products[unit] = result_pool.tile(
+                        [P, BATCH], F32, name="product", align_bytes=64
+                    )
+                    form_product(unit, products[unit][:], sums[1][:], gate_tiles[unit][:])
+            for k in range(len(weights) * STRIDED_UNITS, min(done + 2 * RUN_WEIGHTS, UNITS * len(weights))):
+                if k % len(weights) >= VECTOR_ORDERS and k not in ordered:
+                    order_weight(k, nc.scalar.copy)
+            while quantised < done // 2:
+                quantise_gate(quantised // 2, quantised % 2)
+                quantised += 1
+            unit = min(products) if products else UNITS
+            if unit < VECTOR_TURNS and (unit + 1) * GATES * STEPS + 2 <= run.stop:
+                turn_on_vector(unit, products.pop(unit))
+            elif unit in turned_banks:
+                store_turned(unit, turned_banks[unit], range(BATCH_TILES))
+                products.pop(unit)
 
-        product = None
-        next_ordered = None
-        for unit in range(UNITS):
-            last = unit == UNITS - 1
-            last_product = product
-            ordered = next_ordered
-            codes, scales = this_unit[1:]
-            if not last:
-                next_unit = new_unit()
-                transpose_gate(unit + 1, 0, next_unit[0], ordered)
-            if unit + 2 < UNITS:
-                next_ordered = order_unit(unit + 2)
-            gate_sums = sum_banks.tile([P, BATCH], F32, name="gate_sums")
-            multiply(gate_sums[:], 0, codes, scales)
-            gate_tile = result_pool.tile([P, BATCH], F32, name="gate_tile")
-            nc.scalar.activation(
-                out=gate_tile[:], in_=gate_sums[:], func=SIGMOID, bias=bias[:, 0, unit : unit + 1]
-            )
-            if not last:
-                transpose_gate(unit + 1, 1, next_unit[0], ordered)
-            if unit > VECTOR_TURNS:
-                turned_bank = turn_on_tensor(last_product, range(BATCH_TILES))
-            if unit + 2 < UNITS:
-                order_weights(
-                    unit + 2, next_ordered, slice(VECTOR_ORDERS, len(weights)), nc.scalar.copy
-                )
-            product = result_pool.tile([P, BATCH], F32, name="product", align_bytes=64)
-            if last:
-                half = BATCH // 2
-                for columns, name in (
-                    (slice(0, half), "candidate_sums"),
-                    (slice(half, BATCH), "gate_sums"),
-                ):
-                    sums = sum_banks.tile([P, BATCH], F32, name=name)
-                    multiply(sums[:, :half], 1, codes, scales, columns)
-                    if name == "candidate_sums":
-                        store_turned(unit - 1, turned_bank, range(BATCH_TILES))
-                    form_product(unit, product[:, columns], sums[:, :half], gate_tile[:, columns])
+        unit = UNITS - 1
+        store_turned(unit - 1, turn_on_tensor(products[unit - 1], range(BATCH_TILES)), range(BATCH_TILES))
+        product = result_pool.tile([P, BATCH], F32, name="product", align_bytes=64)
+        pieces = (range(0, 2), range(2, 3), range(3, 4))
+        for i, tiles in enumerate(pieces):
+            columns = slice(tiles.start * P, tiles.stop * P)
+            count = len(tiles) * P
+            if i < GATES:
+                piece_sums = sum_banks.tile([P, BATCH], F32, name="sums_%d" % (1 - i))[:, :count]
             else:
-                sums = sum_banks.tile([P, BATCH], F32, name="candidate_sums")
-                multiply(sums[:], 1, codes, scales)
-                if unit > VECTOR_TURNS:
-                    store_turned(unit - 1, turned_bank, range(BATCH_TILES))
-                elif unit > 0:
-                    turn_on_vector(unit - 1, last_product)
-                for gate in range(GATES):
-                    quantise_gate(gate, *next_unit)
-                form_product(unit, product[:], sums[:], gate_tile[:])
-                this_unit = next_unit
-        for tiles in (range(0, 2), range(2, 4)):
-            store_turned(UNITS - 1, turn_on_tensor(product, tiles), tiles)
+                piece_sums = word_banks.tile([P, WORD_BLOCKS, P], F32, name="bank")[:, 0]
+            for step in range(STEPS):
+                multiply(piece_sums, unit, 1, step, columns)
+            form_product(unit, product[:, columns], piece_sums, gate_tiles[unit][:, columns])
+        for i, tiles in enumerate(pieces):
+            copy = nc.scalar.copy if i == 0 else nc.vector.tensor_copy
+            store_turned(unit, turn_on_tensor(product, tiles), tiles, copy)

@@ -25,11 +25,12 @@ SOURCES = 2
 HALVES = 2
 GATES = 2
 STEPS = SOURCES * PASSES
-RUN_WEIGHTS = 3
-RUN_PASSES = 6
+ORDER_LEAD = 4
+RUN_WEIGHTS = 2
+RUN_PASSES = 4
 STRIDED_UNITS = 2
 BLOCK = 32
-VECTOR_TURNS = 5
+VECTOR_TURNS = 4
 VECTOR_ORDERS = 3
 
 FLOPS = 2 * BATCH * OUTPUTS * FEATURES * SOURCES * GATES
@@ -50,7 +51,7 @@ def tile_lstmcell_pa_kernel(
         act_rows_pool = ctx.enter_context(tc.tile_pool(name="act_rows", bufs=SOURCES))
         w_rows_pool = ctx.enter_context(tc.tile_pool(name="w_rows", bufs=UNITS))
         act_grouped_pool = ctx.enter_context(tc.tile_pool(name="act_grouped", bufs=SOURCES * HALVES))
-        w_ordered_pool = ctx.enter_context(tc.tile_pool(name="w_ordered", bufs=2 * RUN_WEIGHTS + 2))
+        w_ordered_pool = ctx.enter_context(tc.tile_pool(name="w_ordered", bufs=ORDER_LEAD + RUN_WEIGHTS + 1))
         w_grouped_pool = ctx.enter_context(tc.tile_pool(name="w_grouped", bufs=3))
         w_mx_pool = ctx.enter_context(tc.tile_pool(name="w_mx", bufs=3))
         rows_pool = ctx.enter_context(tc.tile_pool(name="rows", bufs=5))
@@ -262,20 +263,19 @@ def tile_lstmcell_pa_kernel(
             range(n, min(n + RUN_PASSES, passes)) for n in range(STEPS, passes, RUN_PASSES)
         ]
         for run in runs:
-            weights_of_run = RUN_WEIGHTS if run.start > 0 else 4
+            weights_of_run = RUN_WEIGHTS if run.start > 0 else 2
             new = range(done, min(done + weights_of_run, UNITS * len(weights)))
             done = new.stop
             for k in new:
                 next_weight(k)
             unit = min(products) if products else UNITS
-            if VECTOR_TURNS <= unit < UNITS - 2:
+            if VECTOR_TURNS <= unit < UNITS - 2 and run.start // STEPS % GATES == 1:
                 turned_banks[unit] = turn_on_tensor(products[unit], range(BATCH_TILES))
-            soon = [
-                k for k in range(done, min(done + RUN_WEIGHTS, UNITS * len(weights)))
-                if k >= STRIDED_UNITS * len(weights)
-            ]
+            soon = range(
+                len(weights) * STRIDED_UNITS, min(done + ORDER_LEAD, UNITS * len(weights))
+            )
             for k in soon:
-                if k % len(weights) < VECTOR_ORDERS:
+                if k % len(weights) < VECTOR_ORDERS and k not in ordered:
                     order_weight(k, nc.vector.tensor_copy)
             for n in run:
                 unit, gate, step = n // (GATES * STEPS), n // STEPS % GATES, n % STEPS
@@ -299,7 +299,7 @@ def tile_lstmcell_pa_kernel(
                         [P, BATCH], F32, name="product", align_bytes=64
                     )
                     form_product(unit, products[unit][:], sums[1][:], gate_tiles[unit][:])
-            for k in range(len(weights) * STRIDED_UNITS, min(done + 2 * RUN_WEIGHTS, UNITS * len(weights))):
+            for k in soon:
                 if k % len(weights) >= VECTOR_ORDERS and k not in ordered:
                     order_weight(k, nc.scalar.copy)
             while quantised < done // 2:

@@ -30,7 +30,7 @@ RUN_WEIGHTS = 2
 RUN_PASSES = 4
 STRIDED_UNITS = 2
 BLOCK = 32
-VECTOR_TURNS = 4
+VECTOR_TURNS = 6
 VECTOR_ORDERS = 3
 
 FLOPS = 2 * BATCH * OUTPUTS * FEATURES * SOURCES * GATES

@@ -301,7 +301,7 @@ def tile_lstmcell_pa_kernel(
                     form_product(unit, products[unit][:], sums[1][:], gate_tiles[unit][:])
             for k in soon:
                 if k % len(weights) >= VECTOR_ORDERS and k not in ordered:
-                    order_weight(k, nc.scalar.copy)
+                    order_weight(k, nc.gpsimd.tensor_copy)
             while quantised < done // 2:
                 quantise_gate(quantised // 2, quantised % 2)
                 quantised += 1

@@ -28,10 +28,9 @@ STEPS = SOURCES * PASSES
 ORDER_LEAD = 4
 RUN_WEIGHTS = 2
 RUN_PASSES = 4
-STRIDED_UNITS = 2
+STRIDED_WEIGHTS = 6
 BLOCK = 32
 VECTOR_TURNS = 6
-VECTOR_ORDERS = 3
 
 FLOPS = 2 * BATCH * OUTPUTS * FEATURES * SOURCES * GATES
 
@@ -51,7 +50,7 @@ def tile_lstmcell_pa_kernel(
         act_rows_pool = ctx.enter_context(tc.tile_pool(name="act_rows", bufs=SOURCES))
         w_rows_pool = ctx.enter_context(tc.tile_pool(name="w_rows", bufs=UNITS))
         act_grouped_pool = ctx.enter_context(tc.tile_pool(name="act_grouped", bufs=SOURCES * HALVES))
-        w_ordered_pool = ctx.enter_context(tc.tile_pool(name="w_ordered", bufs=ORDER_LEAD + RUN_WEIGHTS + 1))
+        w_ordered_pool = ctx.enter_context(tc.tile_pool(name="w_ordered", bufs=ORDER_LEAD + 2 * RUN_WEIGHTS + 1))
         w_grouped_pool = ctx.enter_context(tc.tile_pool(name="w_grouped", bufs=3))
         w_mx_pool = ctx.enter_context(tc.tile_pool(name="w_mx", bufs=3))
         rows_pool = ctx.enter_context(tc.tile_pool(name="rows", bufs=5))
@@ -256,6 +255,9 @@ def tile_lstmcell_pa_kernel(
             out=bias[:], in0=bias_columns[:, :, 0, :], in1=bias_columns[:, :, 1, :], op=ADD
         )
 
+        for k in range(STRIDED_WEIGHTS, 2 * len(weights)):
+            order_weight(k, nc.gpsimd.tensor_copy)
+
         done = len(weights)
         quantised = GATES
         passes = UNITS * GATES * STEPS
@@ -272,10 +274,10 @@ def tile_lstmcell_pa_kernel(
             if VECTOR_TURNS <= unit < UNITS - 2 and run.start // STEPS % GATES == 1:
                 turned_banks[unit] = turn_on_tensor(products[unit], range(BATCH_TILES))
             soon = range(
-                len(weights) * STRIDED_UNITS, min(done + ORDER_LEAD, UNITS * len(weights))
+                STRIDED_WEIGHTS, min(done + ORDER_LEAD, UNITS * len(weights))
             )
             for k in soon:
-                if k % len(weights) < VECTOR_ORDERS and k not in ordered:
+                if k % 2 == 0 and k not in ordered:
                     order_weight(k, nc.vector.tensor_copy)
             for n in run:
                 unit, gate, step = n // (GATES * STEPS), n // STEPS % GATES, n % STEPS
@@ -300,8 +302,8 @@ def tile_lstmcell_pa_kernel(
                     )
                     form_product(unit, products[unit][:], sums[1][:], gate_tiles[unit][:])
             for k in soon:
-                if k % len(weights) >= VECTOR_ORDERS and k not in ordered:
-                    order_weight(k, nc.gpsimd.tensor_copy)
+                if k not in ordered:
+                    order_weight(k, nc.scalar.copy if k % 4 == 1 else nc.gpsimd.tensor_copy)
             while quantised < done // 2:
                 quantise_gate(quantised // 2, quantised % 2)
                 quantised += 1

from contextlib import ExitStack

import concourse.mybir as mybir
from concourse.masks import make_identity

F32 = mybir.dt.float32
BF16 = mybir.dt.bfloat16
U32 = mybir.dt.uint32
U8 = mybir.dt.uint8
FP8X4 = mybir.dt.float8_e4m3fn_x4
SIGMOID = mybir.ActivationFunctionType.Sigmoid
ADD = mybir.AluOpType.add
MULT = mybir.AluOpType.mult

P = 128
PACK = 4
BATCH = 512
FEATURES = 1024
OUTPUTS = 1024
PASSES = FEATURES // (P * PACK)
WORD_BLOCKS = FEATURES // 2 // P
BATCH_TILES = BATCH // P
UNITS = OUTPUTS // P
SOURCES = 2
HALVES = 2
GATES = 2
STEPS = SOURCES * PASSES
ORDER_LEAD = 4
RUN_WEIGHTS = 2
RUN_PASSES = 4
STRIDED_WEIGHTS = 6
BLOCK = 32
VECTOR_TURNS = 6

FLOPS = 2 * BATCH * OUTPUTS * FEATURES * SOURCES * GATES


def tile_lstmcell_pa_kernel(
    tc, incoming, h, W_i, b_W_i, W_c, b_W_c, U_i, b_U_i, U_c, b_U_c, out
):
    nc = tc.nc
    activations = (incoming, h)
    weights = (W_i, U_i, W_c, U_c)
    biases = (b_W_i, b_U_i, b_W_c, b_U_c)

    with ExitStack() as ctx:
        ctx.enter_context(tc.manual_schedule())

        const = ctx.enter_context(tc.tile_pool(name="const", bufs=1))
        act_rows_pool = ctx.enter_context(tc.tile_pool(name="act_rows", bufs=SOURCES))
        w_rows_pool = ctx.enter_context(tc.tile_pool(name="w_rows", bufs=UNITS))
        act_grouped_pool = ctx.enter_context(tc.tile_pool(name="act_grouped", bufs=SOURCES * HALVES))
        w_ordered_pool = ctx.enter_context(tc.tile_pool(name="w_ordered", bufs=ORDER_LEAD + 2 * RUN_WEIGHTS + 1))
        w_grouped_pool = ctx.enter_context(tc.tile_pool(name="w_grouped", bufs=3))
        w_mx_pool = ctx.enter_context(tc.tile_pool(name="w_mx", bufs=3))
        rows_pool = ctx.enter_context(tc.tile_pool(name="rows", bufs=5))
        result_pool = ctx.enter_context(tc.tile_pool(name="result", bufs=3))
        word_banks = ctx.enter_context(tc.psum_pool(name="word_banks", bufs=6))
        sum_banks = ctx.enter_context(tc.psum_pool(name="sum_banks", bufs=1))

        act_rows = []
        for source in range(SOURCES):
            rows = act_rows_pool.tile([P, BATCH_TILES, FEATURES], BF16, name="act_rows")
            for bt in range(BATCH_TILES):
                nc.sync.dma_start(
                    out=rows[:, bt, :], in_=activations[source][bt * P : (bt + 1) * P, :]
                )
            act_rows.append(rows)
        w_rows = []
        for unit in range(UNITS):
            rows = w_rows_pool.tile([P, len(weights), FEATURES], BF16, name="w_rows")
            for m in range(len(weights)):
                nc.sync.dma_start(
                    out=rows[:, m, :], in_=weights[m][unit * P : (unit + 1) * P, :]
                )
            w_rows.append(rows)

        bias_rows = const.tile([P, P], BF16, name="bias_rows")
        nc.vector.memset(bias_rows[:], 0.0)
        for m in range(len(biases)):
            nc.scalar.dma_start(
                out=bias_rows[m * UNITS : (m + 1) * UNITS, :],
                in_=biases[m].rearrange("(u p) -> u p", p=P),
            )

        identity = const.tile([P, P], F32, name="identity")
        make_identity(nc, identity[:])

        warm = const.tile([P, 2], F32, name="warm")
        nc.vector.memset(warm[:], 0.0)
        nc.scalar.activation(out=warm[:, 1:2], in_=warm[:, 0:1], func=SIGMOID)

        def every_second_word(rows_bf16):
            words = rows_bf16.bitcast(F32)
            return [
                words[:, 2 * P * g + u : 2 * P * (g + 1) : 2]
                for g in range(PASSES)
                for u in range(2)
            ]

        def transpose_blocks(blocks, grouped_words, copy):
            bank = word_banks.tile([P, WORD_BLOCKS, P], F32, name="bank")
            for v in range(WORD_BLOCKS):
                nc.tensor.transpose(bank[:, v, :], blocks[v], identity[:])
            copy(out=grouped_words, in_=bank[:].rearrange("p (g u) r -> p g r u", u=2))

        act_codes = const.tile([P, SOURCES, PASSES, BATCH], U32, name="act_codes", align_bytes=64)
        act_scales = const.tile([P, SOURCES, PASSES, BATCH], U8, name="act_scales", align_bytes=64)

        def prepare_activation(source):
            for half in range(HALVES):
                grouped = act_grouped_pool.tile(
                    [P, PASSES, BATCH // HALVES, PACK], BF16, name="act_grouped", align_bytes=64
                )
                grouped_words = grouped[:].bitcast(F32)
                for i in range(BATCH_TILES // HALVES):
                    bt = half * (BATCH_TILES // HALVES) + i
                    transpose_blocks(
                        every_second_word(act_rows[source][:, bt, :]),
                        grouped_words[:, :, i * P : (i + 1) * P, :],
                        nc.vector.tensor_copy if bt == 0 else nc.scalar.copy,
                    )
                columns = slice(half * BATCH // HALVES, (half + 1) * BATCH // HALVES)
                for g in range(PASSES):
                    nc.vector.quantize_mx(
                        out=act_codes[:, source, g, columns].bitcast(FP8X4),
                        scales=act_scales[:, source, g, columns],
                        in_=grouped[:, g].rearrange("p b t -> p (b t)"),
                    )

        prepare_activation(0)

        bias_rows_f32 = const.tile([P, P], F32, name="bias_rows_f32")
        nc.vector.tensor_copy(out=bias_rows_f32[:], in_=bias_rows[:])

        prepare_activation(1)

        def order_weight(k, copy):
            unit, m = divmod(k, len(weights))
            ordered[k] = w_ordered_pool.tile([P, PASSES, 2, P], F32, name="w_ordered")
            copy(
                out=ordered[k][:],
                in_=w_rows[unit][:, m].bitcast(F32).rearrange("r (g p u) -> r g u p", p=P, u=2),
            )

        def transpose_weight(unit, m):
            grouped = units[unit][0]
            k = unit * len(weights) + m
            if k in ordered:
                blocks = [ordered[k][:, g, u, :] for g in range(PASSES) for u in range(2)]
            else:
                blocks = every_second_word(w_rows[unit][:, m, :])
            transpose_blocks(blocks, grouped[:].bitcast(F32)[:, m], nc.scalar.copy)

        def new_unit():
            grouped = w_grouped_pool.tile(
                [P, len(weights), PASSES, P, PACK], BF16, name="w_grouped", align_bytes=64
            )
            codes = w_mx_pool.tile(
                [P, len(weights), PASSES, P], U32, name="w_codes", align_bytes=64
            )
            scales = w_mx_pool.tile(
                [P, len(weights), PASSES, P], U8, name="w_scales", align_bytes=64
            )
            return grouped, codes, scales

        def quantise_gate(unit, gate):
            grouped, codes, scales = units[unit]
            pair = slice(SOURCES * gate, SOURCES * (gate + 1))
            nc.vector.quantize_mx(
                out=codes[:, pair].rearrange("p m g r -> p (m g r)").bitcast(FP8X4),
                scales=scales[:, pair].rearrange("p m g r -> p (m g r)"),
                in_=grouped[:, pair].rearrange("p m g r t -> p (m g r t)"),
            )

        def multiply(sums, unit, gate, step, columns=slice(0, BATCH)):
            codes, scales = units[unit][1:]
            source, g = divmod(step, PASSES)
            m = SOURCES * gate + source
            nc.tensor.matmul_mx(
                out=sums,
                lhsT=codes[:, m, g, :].bitcast(FP8X4),
                lhsT_scale=scales[:, m, g, :],
                rhs=act_codes[:, source, g, columns].bitcast(FP8X4),
                rhs_scale=act_scales[:, source, g, columns],
                start=step == 0,
                stop=step == STEPS - 1,
            )

        def form_product(unit, product, candidate_sums, gate_tile):
            nc.vector.scalar_tensor_tensor(
                out=product,
                in0=candidate_sums,
                scalar=bias[:, 1, unit : unit + 1],
                in1=gate_tile,
                op0=ADD,
                op1=MULT,
            )

        def turn_on_vector(unit, product):
            turned = result_pool.tile([P, BATCH], F32, name="turned", align_bytes=64)
            nc.vector.transpose(out=turned[:], in_=product[:])
            for a in range(P // BLOCK):
                first = unit * P + a * BLOCK
                nc.sync.dma_start(
                    out=out.rearrange("(c i) n -> i c n", i=BLOCK)[:, :, first : first + BLOCK],
                    in_=turned[a * BLOCK : (a + 1) * BLOCK, :].rearrange(
                        "i (c j) -> i c j", j=BLOCK
                    ),
                )

        def turn_on_tensor(product, tiles):
            bank = word_banks.tile([P, WORD_BLOCKS, P], F32, name="bank")
            for i, bt in enumerate(tiles):
                nc.tensor.transpose(bank[:, i, :], product[:, bt * P : (bt + 1) * P], identity[:])
            return bank

        def store_turned(unit, bank, tiles, copy=nc.vector.tensor_copy):
            count = len(tiles)
            rows = rows_pool.tile([P, BATCH_TILES, P], F32, name="rows")
            copy(out=rows[:, :count], in_=bank[:, :count])
            nc.sync.dma_start(
                out=out.rearrange("(c p) n -> p c n", p=P)[
                    :, tiles[0] : tiles[0] + count, unit * P : (unit + 1) * P
                ],
                in_=rows[:, :count],
            )

        units = {}
        ordered = {}
        gate_tiles = {}
        products = {}
        sums = {}
        turned_banks = {}

        def next_weight(k):
            unit, m = divmod(k, len(weights))
            if m == 0:
                units[unit] = new_unit()
            transpose_weight(unit, m)

        for k in range(len(weights)):
            next_weight(k)
            if k % 2 == 1:
                quantise_gate(0, k // 2)
        bias_bank = word_banks.tile([P, WORD_BLOCKS, P], F32, name="bank")
        nc.tensor.transpose(bias_bank[:, 0, :], bias_rows_f32[:], identity[:])
        bias_columns = const.tile([P, GATES, SOURCES, UNITS], F32, name="bias_columns")
        nc.vector.tensor_copy(
            out=bias_columns[:].rearrange("p g s u -> p (g s u)"),
            in_=bias_bank[:, 0, 0 : len(biases) * UNITS],
        )
        bias = const.tile([P, GATES, UNITS], F32, name="bias")
        nc.vector.tensor_tensor(
            out=bias[:], in0=bias_columns[:, :, 0, :], in1=bias_columns[:, :, 1, :], op=ADD
        )

        for k in range(STRIDED_WEIGHTS, 2 * len(weights)):
            order_weight(k, nc.gpsimd.tensor_copy)

        done = len(weights)
        quantised = GATES
        passes = UNITS * GATES * STEPS
        runs = [range(0, STEPS)] + [
            range(n, min(n + RUN_PASSES, passes)) for n in range(STEPS, passes, RUN_PASSES)
        ]
        for run in runs:
            weights_of_run = RUN_WEIGHTS if run.start > 0 else 2
            new = range(done, min(done + weights_of_run, UNITS * len(weights)))
            done = new.stop
            for k in new:
                next_weight(k)
            unit = min(products) if products else UNITS
            if VECTOR_TURNS <= unit < UNITS - 2 and run.start // STEPS % GATES == 1:
                turned_banks[unit] = turn_on_tensor(products[unit], range(BATCH_TILES))
            soon = range(
                STRIDED_WEIGHTS, min(done + ORDER_LEAD, UNITS * len(weights))
            )
            for k in soon:
                if k % 2 == 0 and k not in ordered:
                    order_weight(k, nc.vector.tensor_copy)
            for n in run:
                unit, gate, step = n // (GATES * STEPS), n // STEPS % GATES, n % STEPS
                if unit == UNITS - 1 and gate == 1:
                    break
                if step == 0:
                    sums[gate] = sum_banks.tile([P, BATCH], F32, name="sums_%d" % gate)
                multiply(sums[gate][:], unit, gate, step)
                if step < STEPS - 1:
                    continue
                if gate == 0:
                    gate_tiles[unit] = result_pool.tile([P, BATCH], F32, name="gate_tile")
                    nc.scalar.activation(
                        out=gate_tiles[unit][:],
                        in_=sums[0][:],
                        func=SIGMOID,
                        bias=bias[:, 0, unit : unit + 1],
                    )
                else:
                    products[unit] = result_pool.tile(
                        [P, BATCH], F32, name="product", align_bytes=64
                    )
                    form_product(unit, products[unit][:], sums[1][:], gate_tiles[unit][:])
            for k in soon:
                if k not in ordered:
                    order_weight(k, nc.scalar.copy if k % 4 == 1 else nc.gpsimd.tensor_copy)
            while quantised < done // 2:
                quantise_gate(quantised // 2, quantised % 2)
                quantised += 1
            unit = min(products) if products else UNITS
            if unit < VECTOR_TURNS and (unit + 1) * GATES * STEPS + 2 <= run.stop:
                turn_on_vector(unit, products.pop(unit))
            elif unit in turned_banks:
                store_turned(unit, turned_banks[unit], range(BATCH_TILES))
                products.pop(unit)

        unit = UNITS - 1
        store_turned(unit - 1, turn_on_tensor(products[unit - 1], range(BATCH_TILES)), range(BATCH_TILES))
        product = result_pool.tile([P, BATCH], F32, name="product", align_bytes=64)
        pieces = (range(0, 2), range(2, 3), range(3, 4))
        for i, tiles in enumerate(pieces):
            columns = slice(tiles.start * P, tiles.stop * P)
            count = len(tiles) * P
            if i < GATES:
                piece_sums = sum_banks.tile([P, BATCH], F32, name="sums_%d" % (1 - i))[:, :count]
            else:
                piece_sums = word_banks.tile([P, WORD_BLOCKS, P], F32, name="bank")[:, 0]
            for step in range(STEPS):
                multiply(piece_sums, unit, 1, step, columns)
            form_product(unit, product[:, columns], piece_sums, gate_tiles[unit][:, columns])
        for i, tiles in enumerate(pieces):
            copy = nc.scalar.copy if i == 0 else nc.vector.tensor_copy
            store_turned(unit, turn_on_tensor(product, tiles), tiles, copy)
